import numpy as np
import ml_dtypes


def mxq(x, axis, fmt="e4m3"):
    dtype, down = {"e4m3": (ml_dtypes.float8_e4m3fn, 7), "e5m2": (ml_dtypes.float8_e5m2, 14)}[fmt]
    v = np.moveaxis(np.asarray(x, np.float32).astype(ml_dtypes.bfloat16).astype(np.float64), axis, -1)
    blocks = v.reshape(v.shape[:-1] + (-1, 32))
    amax = np.abs(blocks).max(-1, keepdims=True)
    byte = np.maximum(np.where(amax > 0, np.frexp(amax)[1] - 1 + 127, 0) - down, 1)
    scale = np.exp2(byte - 127.0)
    codes = (blocks / scale).astype(np.float32).astype(dtype).astype(np.float64)
    return np.moveaxis((codes * scale).reshape(v.shape), -1, axis)


WIDE = False


def mx_kscale(k):
    if not WIDE:
        return np.ones(k)
    levels = np.array([10, -10, 5, -5, 0])
    if k % 512:
        return np.exp2(np.random.permutation(np.resize(levels, k // 32))).repeat(32)
    a = np.empty((k // 512, 16))
    for p in range(k // 512):
        a[p, :8] = np.random.permutation(np.resize(levels, 8))
        for g in range(8):
            far = levels[np.abs(levels - a[p, g]) >= 10]
            a[p, g + 8] = far[np.random.randint(len(far))]
    return np.exp2(a.ravel()).repeat(32)


BF16 = ml_dtypes.bfloat16


def bf(x):
    return np.asarray(x, np.float32).astype(BF16)


def f64(x):
    return np.asarray(x).astype(np.float64)


B, D_IN, D_HID, D_OUT, LAT = 512, 192, 16384, 512, 16
BN_EPS = 1e-5
L2_EPS = 1e-12


def setup_inputs():
    t = mx_kscale(D_HID)
    col_sd = np.exp(0.4 * np.random.standard_normal(D_HID))
    col_mean = 0.5 * np.random.standard_normal(D_HID)
    return {
        "y_lin": bf(np.random.standard_normal((B, D_HID)) * col_sd + col_mean),
        "gamma": bf((1.0 + 0.2 * np.random.standard_normal(D_HID)) * t),
        "beta": bf(0.3 * np.random.standard_normal(D_HID) * t),
        "W2": bf(np.random.standard_normal((D_OUT, D_HID)) / np.sqrt(D_HID) / t[None, :]),
        "b2": bf(0.2 * np.random.standard_normal(D_OUT)),
    }


def reference(y_lin, gamma, beta, W2, b2):
    y = f64(y_lin)
    mean = np.mean(y, axis=0)
    var = np.mean((y - mean) ** 2, axis=0)
    y = (y - mean) * (1.0 / np.sqrt(var + BN_EPS)) * f64(gamma) + f64(beta)
    a = np.maximum(y, 0.0)
    p = (mxq(a, 1, "e4m3") @ mxq(f64(W2), 1, "e4m3").T) + f64(b2)
    n = np.sqrt(np.sum(p * p, axis=1, keepdims=True))
    return p / np.maximum(n, L2_EPS)

@@ -1,0 +1,276 @@
+from contextlib import ExitStack
+
+import concourse.mybir as mybir
+from concourse.masks import make_identity
+
+F32 = mybir.dt.float32
+BF16 = mybir.dt.bfloat16
+U32 = mybir.dt.uint32
+U8 = mybir.dt.uint8
+FP8X4 = mybir.dt.float8_e4m3fn_x4
+ALU = mybir.AluOpType
+ACT = mybir.ActivationFunctionType
+
+P = 128
+BATCH = 512
+HIDDEN = 16384
+WIDTH = 512
+ROW_TILES = 4
+PACK = 4
+K_PASS = P * PACK
+N_PASS = HIDDEN // K_PASS
+HALVES = 2
+PAIR = 2
+PASS_WORDS = K_PASS // PAIR
+ROUND_PASSES = 2
+ROUND_K = ROUND_PASSES * K_PASS
+N_ROUNDS = N_PASS // ROUND_PASSES
+ROUND_PLANES = ROUND_PASSES * HALVES
+BN_EPS = 1e-5
+L2_EPS = 1e-12
+STATS_MAX = 512
+RUN = 4
+
+STATS_LEAD = 4
+WEIGHT_LEAD = 2
+PACK_LAG = 1
+MATMUL_LAG = 2
+LOAD_AHEAD = 2
+
+FLOPS = 2 * BATCH * WIDTH * HIDDEN
+
+
+def tile_simclr_pa_k_kernel(tc, y_lin, gamma, beta, W2, b2, out):
+    nc = tc.nc
+    with ExitStack() as ctx:
+        ctx.enter_context(tc.manual_schedule())
+        const = ctx.enter_context(tc.tile_pool(name="const", bufs=1))
+        y_pool = ctx.enter_context(tc.tile_pool(name="y_rows", bufs=6))
+        w_pool = ctx.enter_context(tc.tile_pool(name="w_rows", bufs=4))
+        stat_pool = ctx.enter_context(tc.tile_pool(name="statistics", bufs=3))
+        affine_pool = ctx.enter_context(tc.tile_pool(name="affine", bufs=4))
+        stage = ctx.enter_context(tc.tile_pool(name="stage", bufs=3))
+        y_mx = ctx.enter_context(tc.tile_pool(name="y_mx", bufs=3))
+        w_mx = ctx.enter_context(tc.tile_pool(name="w_mx", bufs=6))
+        tail = ctx.enter_context(tc.tile_pool(name="tail", bufs=ROW_TILES))
+        acc_pool = ctx.enter_context(tc.psum_pool(name="acc", bufs=1))
+        vector_banks = ctx.enter_context(tc.psum_pool(name="vector_banks", bufs=2))
+        scalar_banks = ctx.enter_context(tc.psum_pool(name="scalar_banks", bufs=2))
+
+        y_rows = {}
+        w_rows = {}
+        stats = {}
+        scale = {}
+        shift = {}
+        planes = {}
+        y_codes = {}
+        y_scales = {}
+        w_grouped = {}
+        w_codes = {}
+        w_scales = {}
+
+        def load_round(pool, source, r):
+            rows = pool.tile([P, ROW_TILES, ROUND_K], BF16, tag="rows")
+            nc.sync.dma_start(
+                out=rows[:],
+                in_=source.rearrange("(t p) k -> p t k", p=P)[:, :, r * ROUND_K : (r + 1) * ROUND_K],
+            )
+            return rows
+
+        def transpose_words(dest, rows, t, g, u):
+            first = (g % ROUND_PASSES) * PASS_WORDS
+            nc.tensor.transpose(
+                dest, rows[:].bitcast(F32)[:, t, first + u : first + PASS_WORDS : HALVES], identity[:]
+            )
+
+        def transposed_y(banks, g, u):
+            bank = banks.tile([P, BATCH], F32, tag="bank")
+            for t in range(ROW_TILES):
+                transpose_words(bank[:, t * P : (t + 1) * P], y_rows[g // ROUND_PASSES], t, g, u)
+            return bank
+
+        def read_statistics(g):
+            r = g // ROUND_PASSES
+            if g % ROUND_PASSES == 0:
+                six = stat_pool.tile([P, ROUND_PLANES, 2, 6], F32, tag="six")
+                stats[r] = six
+            for u in range(HALVES):
+                bank = transposed_y(vector_banks, g, u)
+                values = bank[:].bitcast(BF16)
+                for h in range(2):
+                    nc.vector.bn_stats(
+                        out=stats[r][:, (g % ROUND_PASSES) * HALVES + u, h, :],
+                        in_=values[:, h * STATS_MAX : (h + 1) * STATS_MAX],
+                    )
+
+        def finish_statistics(r):
+            shape = [P, ROUND_PLANES, PAIR]
+            gamma_r = gamma_beta[:, 0, r * ROUND_PLANES : (r + 1) * ROUND_PLANES, :]
+            beta_r = gamma_beta[:, 1, r * ROUND_PLANES : (r + 1) * ROUND_PLANES, :]
+            by_parity = stats[r][:].rearrange("p q h (e s) -> p q h e s", s=3)
+            mean_a = by_parity[:, :, 0, :, 1]
+            mean_b = by_parity[:, :, 1, :, 1]
+            dev_a = by_parity[:, :, 0, :, 2]
+            dev_b = by_parity[:, :, 1, :, 2]
+            gap = stat_pool.tile(shape, F32, tag="gap")
+            twice_mean = stat_pool.tile(shape, F32, tag="twice_mean")
+            dev = stat_pool.tile(shape, F32, tag="dev")
+            four_var = stat_pool.tile(shape, F32, tag="four_var")
+            half_rstd = stat_pool.tile(shape, F32, tag="half_rstd")
+            half_scale = stat_pool.tile(shape, F32, tag="half_scale")
+            scale_r = affine_pool.tile(shape, F32, tag="scale")
+            shift_r = affine_pool.tile(shape, F32, tag="shift")
+            nc.gpsimd.tensor_tensor(out=gap[:], in0=mean_a, in1=mean_b, op=ALU.subtract)
+            nc.gpsimd.tensor_tensor(out=twice_mean[:], in0=mean_a, in1=mean_b, op=ALU.add)
+            nc.gpsimd.tensor_tensor(out=dev[:], in0=dev_a, in1=dev_b, op=ALU.add)
+            nc.gpsimd.tensor_tensor(out=gap[:], in0=gap[:], in1=gap[:], op=ALU.mult)
+            nc.gpsimd.tensor_scalar(
+                out=dev[:], in0=dev[:], scalar1=1.0 / 128.0, scalar2=4.0 * BN_EPS, op0=ALU.mult, op1=ALU.add
+            )
+            nc.gpsimd.tensor_tensor(out=four_var[:], in0=dev[:], in1=gap[:], op=ALU.add)
+            nc.gpsimd.tensor_tensor(out=half_rstd[:], in0=four_var[:], in1=minus_half[:], op=ALU.pow)
+            nc.gpsimd.tensor_tensor(out=half_scale[:], in0=half_rstd[:], in1=gamma_r, op=ALU.mult)
+            nc.gpsimd.tensor_scalar(
+                out=scale_r[:], in0=half_scale[:], scalar1=2.0, scalar2=0.0, op0=ALU.mult, op1=ALU.add
+            )
+            nc.gpsimd.tensor_tensor(out=twice_mean[:], in0=twice_mean[:], in1=half_scale[:], op=ALU.mult)
+            nc.gpsimd.tensor_tensor(out=shift_r[:], in0=beta_r, in1=twice_mean[:], op=ALU.subtract)
+            scale[r] = scale_r
+            shift[r] = shift_r
+
+        def normalise(g):
+            r = g // ROUND_PASSES
+            a_planes = stage.tile([P, PACK, BATCH], BF16, tag="a_planes")
+            for u in range(HALVES):
+                q = (g % ROUND_PASSES) * HALVES + u
+                bank = transposed_y(scalar_banks, g, u)
+                values = bank[:].bitcast(BF16).rearrange("p (b e) -> p b e", e=PAIR)
+                for e in range(PAIR):
+                    nc.scalar.activation(
+                        out=a_planes[:, PAIR * u + e, :],
+                        in_=values[:, :, e],
+                        func=ACT.Relu,
+                        scale=scale[r][:, q, e : e + 1],
+                        bias=shift[r][:, q, e : e + 1],
+                    )
+            planes[g] = a_planes
+
+        def copy_weights(g):
+            grouped = stage.tile([P, WIDTH * PACK], BF16, tag="w_grouped", align_bytes=64)
+            words = grouped[:].bitcast(F32).rearrange("p (o u) -> p o u", u=HALVES)
+            rows_in_bank = WIDTH // 2
+            for h in range(2):
+                bank = scalar_banks.tile([P, BATCH], F32, tag="bank")
+                by_half = bank[:].rearrange("p (u o) -> p u o", u=HALVES)
+                for u in range(HALVES):
+                    for j in range(rows_in_bank // P):
+                        transpose_words(
+                            by_half[:, u, j * P : (j + 1) * P], w_rows[g // ROUND_PASSES], 2 * h + j, g, u
+                        )
+                nc.scalar.copy(
+                    out=words[:, h * rows_in_bank : (h + 1) * rows_in_bank, :],
+                    in_=by_half.rearrange("p u o -> p o u"),
+                )
+            w_grouped[g] = grouped
+
+        def quantise(pool, grouped, width, tag):
+            codes = pool.tile([P, width], U32, tag=tag + "_codes", align_bytes=64)
+            scales = pool.tile([P, width], U8, tag=tag + "_scales", align_bytes=64)
+            nc.vector.quantize_mx(out=codes[:].bitcast(FP8X4), scales=scales[:], in_=grouped)
+            return codes, scales
+
+        def multiply(g):
+            for t in range(ROW_TILES):
+                rows = slice(t * P, (t + 1) * P)
+                nc.tensor.matmul_mx(
+                    out=acc[t][:],
+                    lhsT=y_codes[g][:, rows].bitcast(FP8X4),
+                    lhsT_scale=y_scales[g][:, rows],
+                    rhs=w_codes[g][:].bitcast(FP8X4),
+                    rhs_scale=w_scales[g][:],
+                    start=(g == 0),
+                    stop=(g == N_PASS - 1),
+                )
+
+        for r in range(LOAD_AHEAD):
+            y_rows[r] = load_round(y_pool, y_lin, r)
+            w_rows[r] = load_round(w_pool, W2, r)
+        vectors = const.tile([P, K_PASS], BF16)
+        nc.vector.memset(vectors[:], 0.0)
+        nc.scalar.dma_start(out=vectors[0:N_PASS, :], in_=gamma.rearrange("(r c) -> r c", c=K_PASS))
+        nc.scalar.dma_start(out=vectors[N_PASS : 2 * N_PASS, :], in_=beta.rearrange("(r c) -> r c", c=K_PASS))
+        identity = const.tile([P, P], F32)
+        make_identity(nc, identity[:])
+        minus_half = const.tile([P, ROUND_PLANES, PAIR], F32)
+        nc.vector.memset(minus_half[:], -0.5)
+        one = const.tile([P, 1], F32)
+        nc.vector.memset(one[:], 1.0)
+        nc.scalar.activation(out=one[:], in_=one[:], func=ACT.Sqrt)
+        bank = vector_banks.tile([P, BATCH], F32, tag="bank")
+        for u in range(HALVES):
+            nc.tensor.transpose(
+                bank[:, u * P : (u + 1) * P], vectors[:].bitcast(F32)[:, u:PASS_WORDS:HALVES], identity[:]
+            )
+        gamma_beta = const.tile([P, 2, N_PASS * HALVES, PAIR], F32)
+        by_half = bank[:].bitcast(BF16).rearrange("p (u c e) -> p u c e", u=2 * HALVES, e=PAIR)
+        for v in range(2):
+            for u in range(HALVES):
+                nc.vector.tensor_copy(
+                    out=gamma_beta[:, v, u : N_PASS * HALVES : HALVES, :],
+                    in_=by_half[:, u, v * N_PASS : (v + 1) * N_PASS, :],
+                )
+        acc = [acc_pool.tile([P, WIDTH], F32, name="acc%d" % t) for t in range(ROW_TILES)]
+
+        for i in range(-STATS_LEAD, N_PASS + MATMUL_LAG):
+            g_stats = i + STATS_LEAD
+            g_weight = i + WEIGHT_LEAD
+            if 0 <= g_weight < N_PASS:
+                r = g_weight // ROUND_PASSES + LOAD_AHEAD
+                if g_weight % ROUND_PASSES == 0 and r < N_ROUNDS:
+                    w_rows[r] = load_round(w_pool, W2, r)
+                copy_weights(g_weight)
+            if g_stats < N_PASS:
+                r = g_stats // ROUND_PASSES + LOAD_AHEAD
+                if g_stats % ROUND_PASSES == 0 and r < N_ROUNDS:
+                    y_rows[r] = load_round(y_pool, y_lin, r)
+                read_statistics(g_stats)
+                if g_stats % ROUND_PASSES == ROUND_PASSES - 1:
+                    finish_statistics(g_stats // ROUND_PASSES)
+            if 0 <= i < N_PASS:
+                normalise(i)
+            g = i - PACK_LAG
+            if 0 <= g < N_PASS:
+                a_grouped = stage.tile([P, BATCH, PACK], BF16, tag="a_grouped", align_bytes=64)
+                nc.vector.tensor_copy(
+                    out=a_grouped[:].rearrange("p (c j) t -> p c t j", j=RUN),
+                    in_=planes[g][:].rearrange("p t (c j) -> p c t j", j=RUN),
+                )
+            g_w = g + WEIGHT_LEAD
+            if 0 <= g_w < N_PASS:
+                w_codes[g_w], w_scales[g_w] = quantise(w_mx, w_grouped[g_w][:], WIDTH, "w")
+            if 0 <= g < N_PASS:
+                y_codes[g], y_scales[g] = quantise(
+                    y_mx, a_grouped[:].rearrange("p b t -> p (b t)"), BATCH, "y"
+                )
+            if 0 <= i - MATMUL_LAG:
+                multiply(i - MATMUL_LAG)
+
+        bias_rows = const.tile([P, WIDTH], BF16)
+        nc.sync.dma_start(out=bias_rows[:], in_=b2.partition_broadcast(P))
+        logits = []
+        sum_squares = const.tile([P, ROW_TILES], F32)
+        for t in range(ROW_TILES):
+            p_rows = tail.tile([P, WIDTH], F32, tag="p_rows")
+            nc.vector.tensor_tensor(out=p_rows[:], in0=acc[t][:], in1=bias_rows[:], op=ALU.add)
+            squares = tail.tile([P, WIDTH], F32, tag="squares")
+            nc.scalar.activation(
+                out=squares[:], in_=p_rows[:], func=ACT.Square, accum_out=sum_squares[:, t : t + 1]
+            )
+            logits.append(p_rows)
+        norm = const.tile([P, ROW_TILES], F32)
+        nc.scalar.activation(out=norm[:], in_=sum_squares[:], func=ACT.Sqrt)
+        nc.vector.tensor_scalar_max(out=norm[:], in0=norm[:], scalar1=L2_EPS)
+        nc.vector.reciprocal(out=norm[:], in_=norm[:])
+        for t in range(ROW_TILES):
+            nc.vector.tensor_scalar_mul(out=logits[t][:], in0=logits[t][:], scalar1=norm[:, t : t + 1])
+            nc.sync.dma_start(out=out[t * P : (t + 1) * P, :], in_=logits[t][:])

@@ -22,16 +22,20 @@ N_PASS = HIDDEN // K_PASS
 HALVES = 2
 PAIR = 2
 PASS_WORDS = K_PASS // PAIR
-ROUND_PASSES = 2
-ROUND_K = ROUND_PASSES * K_PASS
-N_ROUNDS = N_PASS // ROUND_PASSES
+LOAD_PASSES = 2
+LOAD_K = LOAD_PASSES * K_PASS
+N_LOADS = N_PASS // LOAD_PASSES
+ROUND_PASSES = 4
 ROUND_PLANES = ROUND_PASSES * HALVES
 BN_EPS = 1e-5
 L2_EPS = 1e-12
+BF16_MAX = 3.38953139e38
 STATS_MAX = 512
 RUN = 4
+GPSIMD_ROWS = 384
+SCALAR_PLANES = 3
 
-STATS_LEAD = 4
+STATS_LEAD = 6
 WEIGHT_LEAD = 2
 PACK_LAG = 1
 MATMUL_LAG = 2
@@ -45,127 +49,229 @@ def tile_simclr_pa_k_kernel(tc, y_lin, gamma, beta, W2, b2, out):
     with ExitStack() as ctx:
         ctx.enter_context(tc.manual_schedule())
         const = ctx.enter_context(tc.tile_pool(name="const", bufs=1))
-        y_pool = ctx.enter_context(tc.tile_pool(name="y_rows", bufs=6))
+        y_pool = ctx.enter_context(tc.tile_pool(name="y_rows", bufs=4))
         w_pool = ctx.enter_context(tc.tile_pool(name="w_rows", bufs=4))
-        stat_pool = ctx.enter_context(tc.tile_pool(name="statistics", bufs=3))
-        affine_pool = ctx.enter_context(tc.tile_pool(name="affine", bufs=4))
+        word_pool = ctx.enter_context(tc.tile_pool(name="y_words", bufs=STATS_LEAD + 2))
+        stat_pool = ctx.enter_context(tc.tile_pool(name="statistics", bufs=2))
+        affine_pool = ctx.enter_context(tc.tile_pool(name="affine", bufs=3))
         stage = ctx.enter_context(tc.tile_pool(name="stage", bufs=3))
+        group_pool = ctx.enter_context(tc.tile_pool(name="a_grouped", bufs=1))
         y_mx = ctx.enter_context(tc.tile_pool(name="y_mx", bufs=3))
         w_mx = ctx.enter_context(tc.tile_pool(name="w_mx", bufs=6))
         tail = ctx.enter_context(tc.tile_pool(name="tail", bufs=ROW_TILES))
         acc_pool = ctx.enter_context(tc.psum_pool(name="acc", bufs=1))
-        vector_banks = ctx.enter_context(tc.psum_pool(name="vector_banks", bufs=2))
-        scalar_banks = ctx.enter_context(tc.psum_pool(name="scalar_banks", bufs=2))
+        y_banks = ctx.enter_context(tc.psum_pool(name="y_banks", bufs=2))
+        w_banks = ctx.enter_context(tc.psum_pool(name="w_banks", bufs=2))
 
         y_rows = {}
         w_rows = {}
+        y_words = {}
         stats = {}
+        chain = {}
         scale = {}
         shift = {}
         planes = {}
+        a_grouped = {}
         y_codes = {}
         y_scales = {}
         w_grouped = {}
         w_codes = {}
         w_scales = {}
 
-        def load_round(pool, source, r):
-            rows = pool.tile([P, ROW_TILES, ROUND_K], BF16, tag="rows")
-            nc.sync.dma_start(
-                out=rows[:],
-                in_=source.rearrange("(t p) k -> p t k", p=P)[:, :, r * ROUND_K : (r + 1) * ROUND_K],
-            )
+        def load(pool, source, r, pieces=1):
+            rows = pool.tile([P, ROW_TILES, LOAD_K], BF16, tag="rows")
+            width = LOAD_K // pieces
+            for first in range(0, LOAD_K, width):
+                nc.sync.dma_start(
+                    out=rows[:, :, first : first + width],
+                    in_=source.rearrange("(t p) k -> p t k", p=P)[
+                        :, :, r * LOAD_K + first : r * LOAD_K + first + width
+                    ],
+                )
             return rows
 
         def transpose_words(dest, rows, t, g, u):
-            first = (g % ROUND_PASSES) * PASS_WORDS
+            first = (g % LOAD_PASSES) * PASS_WORDS
             nc.tensor.transpose(
                 dest, rows[:].bitcast(F32)[:, t, first + u : first + PASS_WORDS : HALVES], identity[:]
             )
 
-        def transposed_y(banks, g, u):
-            bank = banks.tile([P, BATCH], F32, tag="bank")
-            for t in range(ROW_TILES):
-                transpose_words(bank[:, t * P : (t + 1) * P], y_rows[g // ROUND_PASSES], t, g, u)
-            return bank
-
-        def read_statistics(g):
+        def read_words(g):
             r = g // ROUND_PASSES
             if g % ROUND_PASSES == 0:
                 six = stat_pool.tile([P, ROUND_PLANES, 2, 6], F32, tag="six")
                 stats[r] = six
+            words = word_pool.tile([P, HALVES, BATCH], F32, tag="words")
             for u in range(HALVES):
-                bank = transposed_y(vector_banks, g, u)
+                bank = y_banks.tile([P, BATCH], F32, tag="bank")
+                for t in range(ROW_TILES):
+                    transpose_words(bank[:, t * P : (t + 1) * P], y_rows[g // LOAD_PASSES], t, g, u)
+                nc.scalar.copy(out=words[:, u, :], in_=bank[:])
                 values = bank[:].bitcast(BF16)
                 for h in range(2):
                     nc.vector.bn_stats(
                         out=stats[r][:, (g % ROUND_PASSES) * HALVES + u, h, :],
                         in_=values[:, h * STATS_MAX : (h + 1) * STATS_MAX],
                     )
+            y_words[g] = words
 
-        def finish_statistics(r):
+        def spread_gamma_beta():
+            bank = w_banks.tile([P, BATCH], F32, tag="bank")
+            for u in range(HALVES):
+                nc.tensor.transpose(
+                    bank[:, u * P : (u + 1) * P], vectors[:].bitcast(F32)[:, u:PASS_WORDS:HALVES], identity[:]
+                )
+            by_half = bank[:].bitcast(BF16).rearrange("p (u c e) -> p u c e", u=2 * HALVES, e=PAIR)
+            for v in range(2):
+                for u in range(HALVES):
+                    nc.vector.tensor_copy(
+                        out=gamma_beta[:, v, u : N_PASS * HALVES : HALVES, :],
+                        in_=by_half[:, u, v * N_PASS : (v + 1) * N_PASS, :],
+                    )
+
+        def begin_chain(r):
             shape = [P, ROUND_PLANES, PAIR]
-            gamma_r = gamma_beta[:, 0, r * ROUND_PLANES : (r + 1) * ROUND_PLANES, :]
-            beta_r = gamma_beta[:, 1, r * ROUND_PLANES : (r + 1) * ROUND_PLANES, :]
-            by_parity = stats[r][:].rearrange("p q h (e s) -> p q h e s", s=3)
-            mean_a = by_parity[:, :, 0, :, 1]
-            mean_b = by_parity[:, :, 1, :, 1]
-            dev_a = by_parity[:, :, 0, :, 2]
-            dev_b = by_parity[:, :, 1, :, 2]
             gap = stat_pool.tile(shape, F32, tag="gap")
             twice_mean = stat_pool.tile(shape, F32, tag="twice_mean")
             dev = stat_pool.tile(shape, F32, tag="dev")
-            four_var = stat_pool.tile(shape, F32, tag="four_var")
-            half_rstd = stat_pool.tile(shape, F32, tag="half_rstd")
-            half_scale = stat_pool.tile(shape, F32, tag="half_scale")
+            std = stat_pool.tile(shape, F32, tag="std")
             scale_r = affine_pool.tile(shape, F32, tag="scale")
             shift_r = affine_pool.tile(shape, F32, tag="shift")
-            nc.gpsimd.tensor_tensor(out=gap[:], in0=mean_a, in1=mean_b, op=ALU.subtract)
-            nc.gpsimd.tensor_tensor(out=twice_mean[:], in0=mean_a, in1=mean_b, op=ALU.add)
-            nc.gpsimd.tensor_tensor(out=dev[:], in0=dev_a, in1=dev_b, op=ALU.add)
-            nc.gpsimd.tensor_tensor(out=gap[:], in0=gap[:], in1=gap[:], op=ALU.mult)
-            nc.gpsimd.tensor_scalar(
-                out=dev[:], in0=dev[:], scalar1=1.0 / 128.0, scalar2=4.0 * BN_EPS, op0=ALU.mult, op1=ALU.add
-            )
-            nc.gpsimd.tensor_tensor(out=four_var[:], in0=dev[:], in1=gap[:], op=ALU.add)
-            nc.gpsimd.tensor_tensor(out=half_rstd[:], in0=four_var[:], in1=minus_half[:], op=ALU.pow)
-            nc.gpsimd.tensor_tensor(out=half_scale[:], in0=half_rstd[:], in1=gamma_r, op=ALU.mult)
-            nc.gpsimd.tensor_scalar(
-                out=scale_r[:], in0=half_scale[:], scalar1=2.0, scalar2=0.0, op0=ALU.mult, op1=ALU.add
-            )
-            nc.gpsimd.tensor_tensor(out=twice_mean[:], in0=twice_mean[:], in1=half_scale[:], op=ALU.mult)
-            nc.gpsimd.tensor_tensor(out=shift_r[:], in0=beta_r, in1=twice_mean[:], op=ALU.subtract)
+            chain[r] = gap, twice_mean, dev, std
             scale[r] = scale_r
             shift[r] = shift_r
 
-        def normalise(g):
+        def moments(r):
+            by_parity = stats[r][:].rearrange("p q h (e s) -> p q h e s", s=3)
+            return [by_parity[:, :, h, :, s] for s in (1, 2) for h in range(2)]
+
+        def chain_a(r):
+            begin_chain(r)
+            mean_a, mean_b, dev_a, dev_b = moments(r)
+            gap, twice_mean, dev, std = chain[r]
+            nc.vector.tensor_tensor(out=gap[:], in0=mean_a, in1=mean_b, op=ALU.subtract)
+            nc.vector.tensor_tensor(out=dev[:], in0=dev_a, in1=dev_b, op=ALU.add)
+
+        def chain_b(r):
+            mean_a, mean_b, dev_a, dev_b = moments(r)
+            gap, twice_mean, dev, std = chain[r]
+            nc.vector.tensor_tensor(out=gap[:], in0=gap[:], in1=gap[:], op=ALU.mult)
+            nc.vector.tensor_tensor(out=twice_mean[:], in0=mean_a, in1=mean_b, op=ALU.add)
+
+        def chain_c(r):
+            gap, twice_mean, dev, std = chain[r]
+            nc.vector.scalar_tensor_tensor(
+                out=dev[:], in0=dev[:], scalar=1.0 / 128.0, in1=gap[:], op0=ALU.mult, op1=ALU.add
+            )
+
+        def chain_sqrt(r):
+            gap, twice_mean, dev, std = chain[r]
+            nc.scalar.activation(out=std[:], in_=dev[:], func=ACT.Sqrt, scale=0.25, bias=eps[:])
+
+        def chain_d(r):
+            gap, twice_mean, dev, std = chain[r]
+            nc.vector.reciprocal(out=std[:], in_=std[:])
+
+        def chain_e(r):
+            gap, twice_mean, dev, std = chain[r]
+            gamma_r = gamma_beta[:, 0, r * ROUND_PLANES : (r + 1) * ROUND_PLANES, :]
+            nc.vector.tensor_tensor(out=scale[r][:], in0=std[:], in1=gamma_r, op=ALU.mult)
+
+        def chain_f(r):
+            gap, twice_mean, dev, std = chain[r]
+            nc.vector.scalar_tensor_tensor(
+                out=gap[:].rearrange("p q e -> p (q e)"),
+                in0=twice_mean[:].rearrange("p q e -> p (q e)"),
+                scalar=0.5,
+                in1=scale[r][:].rearrange("p q e -> p (q e)"),
+                op0=ALU.mult,
+                op1=ALU.mult,
+            )
+
+        def chain_g(r):
+            gap, twice_mean, dev, std = chain[r]
+            beta_r = gamma_beta[:, 1, r * ROUND_PLANES : (r + 1) * ROUND_PLANES, :]
+            nc.vector.tensor_tensor(out=shift[r][:], in0=beta_r, in1=gap[:], op=ALU.subtract)
+
+        links = {
+            (0, 0): (chain_a,),
+            (0, 1): (chain_b,),
+            (0, 2): (chain_c,),
+            (1, 0): (chain_d,),
+            (1, 1): (chain_e,),
+            (1, 2): (chain_f,),
+            (2, 0): (chain_g,),
+        }
+
+        def run_links(g_stats, slot):
+            for late in range(3):
+                g = g_stats - late
+                if 0 <= g < N_PASS and g % ROUND_PASSES == ROUND_PASSES - 1:
+                    for link in links.get((late, slot), ()):
+                        link(g // ROUND_PASSES)
+
+        def scale_shift(g, u, e):
             r = g // ROUND_PASSES
+            q = (g % ROUND_PASSES) * HALVES + u
+            return scale[r][:, q, e : e + 1], shift[r][:, q, e : e + 1]
+
+        def begin_planes(g):
             a_planes = stage.tile([P, PACK, BATCH], BF16, tag="a_planes")
-            for u in range(HALVES):
-                q = (g % ROUND_PASSES) * HALVES + u
-                bank = transposed_y(scalar_banks, g, u)
-                values = bank[:].bitcast(BF16).rearrange("p (b e) -> p b e", e=PAIR)
-                for e in range(PAIR):
-                    nc.scalar.activation(
-                        out=a_planes[:, PAIR * u + e, :],
-                        in_=values[:, :, e],
-                        func=ACT.Relu,
-                        scale=scale[r][:, q, e : e + 1],
-                        bias=shift[r][:, q, e : e + 1],
-                    )
             planes[g] = a_planes
+
+        def word_values(g, u, e):
+            return y_words[g][:].bitcast(BF16).rearrange("p u (b e) -> p u b e", e=PAIR)[:, u, :, e]
+
+        def normalise_scalar(g):
+            for t in range(SCALAR_PLANES):
+                u, e = divmod(t, PAIR)
+                by, to = scale_shift(g, u, e)
+                nc.scalar.activation(
+                    out=planes[g][:, t, :], in_=word_values(g, u, e), func=ACT.Relu, scale=by, bias=to
+                )
+
+        def normalise_vector(g):
+            for t in range(SCALAR_PLANES, PACK):
+                u, e = divmod(t, PAIR)
+                by, to = scale_shift(g, u, e)
+                nc.vector.tensor_scalar(
+                    out=planes[g][:, t, :],
+                    in0=word_values(g, u, e),
+                    scalar1=by,
+                    scalar2=to,
+                    op0=ALU.mult,
+                    op1=ALU.add,
+                )
+
+        def regroup_views(g, first, last):
+            return (
+                a_grouped[g][:, first:last, :].rearrange("p (c j) t -> p c t j", j=RUN),
+                planes[g][:, :, first:last].rearrange("p t (c j) -> p c t j", j=RUN),
+            )
+
+        def regroup_gpsimd(g):
+            grouped = group_pool.tile([P, BATCH, PACK], BF16, tag="grouped", align_bytes=64)
+            a_grouped[g] = grouped
+            dest, source = regroup_views(g, 0, GPSIMD_ROWS)
+            nc.gpsimd.tensor_scalar(
+                out=dest, in0=source, scalar1=BF16_MAX, scalar2=0.0, op0=ALU.min, op1=ALU.max
+            )
+
+        def regroup_vector(g):
+            dest, source = regroup_views(g, GPSIMD_ROWS, BATCH)
+            nc.vector.tensor_scalar_max(out=dest, in0=source, scalar1=0.0)
 
         def copy_weights(g):
             grouped = stage.tile([P, WIDTH * PACK], BF16, tag="w_grouped", align_bytes=64)
             words = grouped[:].bitcast(F32).rearrange("p (o u) -> p o u", u=HALVES)
             rows_in_bank = WIDTH // 2
             for h in range(2):
-                bank = scalar_banks.tile([P, BATCH], F32, tag="bank")
+                bank = w_banks.tile([P, BATCH], F32, tag="bank")
                 by_half = bank[:].rearrange("p (u o) -> p u o", u=HALVES)
                 for u in range(HALVES):
                     for j in range(rows_in_bank // P):
                         transpose_words(
-                            by_half[:, u, j * P : (j + 1) * P], w_rows[g // ROUND_PASSES], 2 * h + j, g, u
+                            by_half[:, u, j * P : (j + 1) * P], w_rows[g // LOAD_PASSES], 2 * h + j, g, u
                         )
                 nc.scalar.copy(
                     out=words[:, h * rows_in_bank : (h + 1) * rows_in_bank, :],
@@ -192,66 +298,58 @@ def tile_simclr_pa_k_kernel(tc, y_lin, gamma, beta, W2, b2, out):
                     stop=(g == N_PASS - 1),
                 )
 
-        for r in range(LOAD_AHEAD):
-            y_rows[r] = load_round(y_pool, y_lin, r)
-            w_rows[r] = load_round(w_pool, W2, r)
-        vectors = const.tile([P, K_PASS], BF16)
-        nc.vector.memset(vectors[:], 0.0)
-        nc.scalar.dma_start(out=vectors[0:N_PASS, :], in_=gamma.rearrange("(r c) -> r c", c=K_PASS))
-        nc.scalar.dma_start(out=vectors[N_PASS : 2 * N_PASS, :], in_=beta.rearrange("(r c) -> r c", c=K_PASS))
+        y_rows[0] = load(y_pool, y_lin, 0, pieces=LOAD_PASSES)
         identity = const.tile([P, P], F32)
         make_identity(nc, identity[:])
-        minus_half = const.tile([P, ROUND_PLANES, PAIR], F32)
-        nc.vector.memset(minus_half[:], -0.5)
+        vectors = const.tile([P, K_PASS], BF16)
+        nc.gpsimd.memset(vectors[2 * N_PASS : P, :], 0.0)
+        nc.sync.dma_start(out=vectors[0:N_PASS, :], in_=gamma.rearrange("(r c) -> r c", c=K_PASS))
+        nc.sync.dma_start(out=vectors[N_PASS : 2 * N_PASS, :], in_=beta.rearrange("(r c) -> r c", c=K_PASS))
+        y_rows[1] = load(y_pool, y_lin, 1)
         one = const.tile([P, 1], F32)
         nc.vector.memset(one[:], 1.0)
+        eps = const.tile([P, 1], F32)
+        nc.vector.tensor_scalar(out=eps[:], in0=one[:], scalar1=BN_EPS, scalar2=None, op0=ALU.mult)
         nc.scalar.activation(out=one[:], in_=one[:], func=ACT.Sqrt)
-        bank = vector_banks.tile([P, BATCH], F32, tag="bank")
-        for u in range(HALVES):
-            nc.tensor.transpose(
-                bank[:, u * P : (u + 1) * P], vectors[:].bitcast(F32)[:, u:PASS_WORDS:HALVES], identity[:]
-            )
         gamma_beta = const.tile([P, 2, N_PASS * HALVES, PAIR], F32)
-        by_half = bank[:].bitcast(BF16).rearrange("p (u c e) -> p u c e", u=2 * HALVES, e=PAIR)
-        for v in range(2):
-            for u in range(HALVES):
-                nc.vector.tensor_copy(
-                    out=gamma_beta[:, v, u : N_PASS * HALVES : HALVES, :],
-                    in_=by_half[:, u, v * N_PASS : (v + 1) * N_PASS, :],
-                )
         acc = [acc_pool.tile([P, WIDTH], F32, name="acc%d" % t) for t in range(ROW_TILES)]
 
         for i in range(-STATS_LEAD, N_PASS + MATMUL_LAG):
             g_stats = i + STATS_LEAD
             g_weight = i + WEIGHT_LEAD
-            if 0 <= g_weight < N_PASS:
-                r = g_weight // ROUND_PASSES + LOAD_AHEAD
-                if g_weight % ROUND_PASSES == 0 and r < N_ROUNDS:
-                    w_rows[r] = load_round(w_pool, W2, r)
-                copy_weights(g_weight)
+            g_pack = i - PACK_LAG
+            g_w = g_pack + WEIGHT_LEAD
+            if 0 <= g_pack < N_PASS:
+                regroup_gpsimd(g_pack)
             if g_stats < N_PASS:
-                r = g_stats // ROUND_PASSES + LOAD_AHEAD
-                if g_stats % ROUND_PASSES == 0 and r < N_ROUNDS:
-                    y_rows[r] = load_round(y_pool, y_lin, r)
-                read_statistics(g_stats)
-                if g_stats % ROUND_PASSES == ROUND_PASSES - 1:
-                    finish_statistics(g_stats // ROUND_PASSES)
-            if 0 <= i < N_PASS:
-                normalise(i)
-            g = i - PACK_LAG
-            if 0 <= g < N_PASS:
-                a_grouped = stage.tile([P, BATCH, PACK], BF16, tag="a_grouped", align_bytes=64)
-                nc.vector.tensor_copy(
-                    out=a_grouped[:].rearrange("p (c j) t -> p c t j", j=RUN),
-                    in_=planes[g][:].rearrange("p t (c j) -> p c t j", j=RUN),
-                )
-            g_w = g + WEIGHT_LEAD
+                r = g_stats // LOAD_PASSES + LOAD_AHEAD
+                if g_stats % LOAD_PASSES == 0 and r < N_LOADS:
+                    y_rows[r] = load(y_pool, y_lin, r)
+                read_words(g_stats)
+                if g_stats == 0:
+                    spread_gamma_beta()
+            if g_stats % ROUND_PASSES == 0 and ROUND_PASSES <= g_stats <= N_PASS:
+                chain_sqrt(g_stats // ROUND_PASSES - 1)
+            r = g_weight // LOAD_PASSES + LOAD_AHEAD
+            if g_weight % LOAD_PASSES == 0 and 0 <= r < N_LOADS:
+                w_rows[r] = load(w_pool, W2, r)
+            if 0 <= g_weight < N_PASS:
+                copy_weights(g_weight)
+            if 0 <= g_pack < N_PASS:
+                regroup_vector(g_pack)
+            run_links(g_stats, 0)
             if 0 <= g_w < N_PASS:
                 w_codes[g_w], w_scales[g_w] = quantise(w_mx, w_grouped[g_w][:], WIDTH, "w")
-            if 0 <= g < N_PASS:
-                y_codes[g], y_scales[g] = quantise(
-                    y_mx, a_grouped[:].rearrange("p b t -> p (b t)"), BATCH, "y"
+            run_links(g_stats, 1)
+            if 0 <= g_pack < N_PASS:
+                y_codes[g_pack], y_scales[g_pack] = quantise(
+                    y_mx, a_grouped[g_pack][:].rearrange("p b t -> p (b t)"), BATCH, "y"
                 )
+            run_links(g_stats, 2)
+            if 0 <= i < N_PASS:
+                begin_planes(i)
+                normalise_scalar(i)
+                normalise_vector(i)
             if 0 <= i - MATMUL_LAG:
                 multiply(i - MATMUL_LAG)
 

@@ -252,7 +252,8 @@ def tile_simclr_pa_k_kernel(tc, y_lin, gamma, beta, W2, b2, out):
         def regroup_gpsimd(g):
             grouped = group_pool.tile([P, BATCH, PACK], BF16, tag="grouped", align_bytes=64)
             a_grouped[g] = grouped
-            dest, source = regroup_views(g, 0, GPSIMD_ROWS)
+            dest = grouped[:, 0:GPSIMD_ROWS, :]
+            source = planes[g][:, :, 0:GPSIMD_ROWS].rearrange("p t c -> p c t")
             nc.gpsimd.tensor_scalar(
                 out=dest, in0=source, scalar1=BF16_MAX, scalar2=0.0, op0=ALU.min, op1=ALU.max
             )

@@ -32,11 +32,11 @@ L2_EPS = 1e-12
 BF16_MAX = 3.38953139e38
 STATS_MAX = 512
 RUN = 4
-GPSIMD_ROWS = 384
+GPSIMD_ROWS = 352
 SCALAR_PLANES = 3
 
 STATS_LEAD = 6
-WEIGHT_LEAD = 2
+WEIGHT_LEAD = 5
 PACK_LAG = 1
 MATMUL_LAG = 2
 LOAD_AHEAD = 2
@@ -57,7 +57,7 @@ def tile_simclr_pa_k_kernel(tc, y_lin, gamma, beta, W2, b2, out):
         stage = ctx.enter_context(tc.tile_pool(name="stage", bufs=3))
         group_pool = ctx.enter_context(tc.tile_pool(name="a_grouped", bufs=1))
         y_mx = ctx.enter_context(tc.tile_pool(name="y_mx", bufs=3))
-        w_mx = ctx.enter_context(tc.tile_pool(name="w_mx", bufs=6))
+        w_mx = ctx.enter_context(tc.tile_pool(name="w_mx", bufs=8))
         tail = ctx.enter_context(tc.tile_pool(name="tail", bufs=ROW_TILES))
         acc_pool = ctx.enter_context(tc.psum_pool(name="acc", bufs=1))
         y_banks = ctx.enter_context(tc.psum_pool(name="y_banks", bufs=2))
@@ -249,17 +249,21 @@ def tile_simclr_pa_k_kernel(tc, y_lin, gamma, beta, W2, b2, out):
                 planes[g][:, :, first:last].rearrange("p t (c j) -> p c t j", j=RUN),
             )
 
+        def beside_statistics(g):
+            return g + PACK_LAG + STATS_LEAD < N_PASS
+
         def regroup_gpsimd(g):
             grouped = group_pool.tile([P, BATCH, PACK], BF16, tag="grouped", align_bytes=64)
             a_grouped[g] = grouped
-            dest = grouped[:, 0:GPSIMD_ROWS, :]
-            source = planes[g][:, :, 0:GPSIMD_ROWS].rearrange("p t c -> p c t")
+            if not beside_statistics(g):
+                return
+            dest, source = regroup_views(g, 0, GPSIMD_ROWS)
             nc.gpsimd.tensor_scalar(
                 out=dest, in0=source, scalar1=BF16_MAX, scalar2=0.0, op0=ALU.min, op1=ALU.max
             )
 
         def regroup_vector(g):
-            dest, source = regroup_views(g, GPSIMD_ROWS, BATCH)
+            dest, source = regroup_views(g, GPSIMD_ROWS if beside_statistics(g) else 0, BATCH)
             nc.vector.tensor_scalar_max(out=dest, in0=source, scalar1=0.0)
 
         def copy_weights(g):
@@ -307,6 +311,8 @@ def tile_simclr_pa_k_kernel(tc, y_lin, gamma, beta, W2, b2, out):
         nc.sync.dma_start(out=vectors[0:N_PASS, :], in_=gamma.rearrange("(r c) -> r c", c=K_PASS))
         nc.sync.dma_start(out=vectors[N_PASS : 2 * N_PASS, :], in_=beta.rearrange("(r c) -> r c", c=K_PASS))
         y_rows[1] = load(y_pool, y_lin, 1)
+        for r in range(LOAD_AHEAD):
+            w_rows[r] = load(w_pool, W2, r)
         one = const.tile([P, 1], F32)
         nc.vector.memset(one[:], 1.0)
         eps = const.tile([P, 1], F32)
@@ -342,34 +348,47 @@ def tile_simclr_pa_k_kernel(tc, y_lin, gamma, beta, W2, b2, out):
             if 0 <= g_w < N_PASS:
                 w_codes[g_w], w_scales[g_w] = quantise(w_mx, w_grouped[g_w][:], WIDTH, "w")
             run_links(g_stats, 1)
+            late = 0 <= i < N_PASS and g_stats >= N_PASS
+            if late:
+                begin_planes(i)
+                normalise_vector(i)
             if 0 <= g_pack < N_PASS:
                 y_codes[g_pack], y_scales[g_pack] = quantise(
                     y_mx, a_grouped[g_pack][:].rearrange("p b t -> p (b t)"), BATCH, "y"
                 )
             run_links(g_stats, 2)
             if 0 <= i < N_PASS:
-                begin_planes(i)
+                if not late:
+                    begin_planes(i)
                 normalise_scalar(i)
-                normalise_vector(i)
+                if not late:
+                    normalise_vector(i)
             if 0 <= i - MATMUL_LAG:
                 multiply(i - MATMUL_LAG)
 
         bias_rows = const.tile([P, WIDTH], BF16)
         nc.sync.dma_start(out=bias_rows[:], in_=b2.partition_broadcast(P))
-        logits = []
-        sum_squares = const.tile([P, ROW_TILES], F32)
-        for t in range(ROW_TILES):
+        logits = {}
+        norms = {}
+
+        def add_bias(t):
             p_rows = tail.tile([P, WIDTH], F32, tag="p_rows")
             nc.vector.tensor_tensor(out=p_rows[:], in0=acc[t][:], in1=bias_rows[:], op=ALU.add)
             squares = tail.tile([P, WIDTH], F32, tag="squares")
-            nc.scalar.activation(
-                out=squares[:], in_=p_rows[:], func=ACT.Square, accum_out=sum_squares[:, t : t + 1]
-            )
-            logits.append(p_rows)
-        norm = const.tile([P, ROW_TILES], F32)
-        nc.scalar.activation(out=norm[:], in_=sum_squares[:], func=ACT.Sqrt)
-        nc.vector.tensor_scalar_max(out=norm[:], in0=norm[:], scalar1=L2_EPS)
-        nc.vector.reciprocal(out=norm[:], in_=norm[:])
-        for t in range(ROW_TILES):
-            nc.vector.tensor_scalar_mul(out=logits[t][:], in0=logits[t][:], scalar1=norm[:, t : t + 1])
+            norm = tail.tile([P, 1], F32, tag="norm")
+            nc.scalar.activation(out=squares[:], in_=p_rows[:], func=ACT.Square, accum_out=norm[:])
+            nc.scalar.activation(out=norm[:], in_=norm[:], func=ACT.Sqrt)
+            logits[t] = p_rows
+            norms[t] = norm
+
+        def divide_by_norm(t):
+            nc.vector.tensor_scalar_max(out=norms[t][:], in0=norms[t][:], scalar1=L2_EPS)
+            nc.vector.reciprocal(out=norms[t][:], in_=norms[t][:])
+            nc.vector.tensor_scalar_mul(out=logits[t][:], in0=logits[t][:], scalar1=norms[t][:])
             nc.sync.dma_start(out=out[t * P : (t + 1) * P, :], in_=logits[t][:])
+
+        for t in range(ROW_TILES + 2):
+            if t < ROW_TILES:
+                add_bias(t)
+            if t >= 2:
+                divide_by_norm(t - 2)

from contextlib import ExitStack

import concourse.mybir as mybir
from concourse.masks import make_identity

F32 = mybir.dt.float32
BF16 = mybir.dt.bfloat16
U32 = mybir.dt.uint32
U8 = mybir.dt.uint8
FP8X4 = mybir.dt.float8_e4m3fn_x4
ALU = mybir.AluOpType
ACT = mybir.ActivationFunctionType

P = 128
BATCH = 512
HIDDEN = 16384
WIDTH = 512
ROW_TILES = 4
PACK = 4
K_PASS = P * PACK
N_PASS = HIDDEN // K_PASS
HALVES = 2
PAIR = 2
PASS_WORDS = K_PASS // PAIR
LOAD_PASSES = 2
LOAD_K = LOAD_PASSES * K_PASS
N_LOADS = N_PASS // LOAD_PASSES
ROUND_PASSES = 4
ROUND_PLANES = ROUND_PASSES * HALVES
BN_EPS = 1e-5
L2_EPS = 1e-12
BF16_MAX = 3.38953139e38
STATS_MAX = 512
RUN = 4
GPSIMD_ROWS = 352
SCALAR_PLANES = 3

STATS_LEAD = 6
WEIGHT_LEAD = 5
PACK_LAG = 1
MATMUL_LAG = 2
LOAD_AHEAD = 2

FLOPS = 2 * BATCH * WIDTH * HIDDEN


def tile_simclr_pa_k_kernel(tc, y_lin, gamma, beta, W2, b2, out):
    nc = tc.nc
    with ExitStack() as ctx:
        ctx.enter_context(tc.manual_schedule())
        const = ctx.enter_context(tc.tile_pool(name="const", bufs=1))
        y_pool = ctx.enter_context(tc.tile_pool(name="y_rows", bufs=4))
        w_pool = ctx.enter_context(tc.tile_pool(name="w_rows", bufs=4))
        word_pool = ctx.enter_context(tc.tile_pool(name="y_words", bufs=STATS_LEAD + 2))
        stat_pool = ctx.enter_context(tc.tile_pool(name="statistics", bufs=2))
        affine_pool = ctx.enter_context(tc.tile_pool(name="affine", bufs=3))
        stage = ctx.enter_context(tc.tile_pool(name="stage", bufs=3))
        group_pool = ctx.enter_context(tc.tile_pool(name="a_grouped", bufs=1))
        y_mx = ctx.enter_context(tc.tile_pool(name="y_mx", bufs=3))
        w_mx = ctx.enter_context(tc.tile_pool(name="w_mx", bufs=8))
        tail = ctx.enter_context(tc.tile_pool(name="tail", bufs=ROW_TILES))
        acc_pool = ctx.enter_context(tc.psum_pool(name="acc", bufs=1))
        y_banks = ctx.enter_context(tc.psum_pool(name="y_banks", bufs=2))
        w_banks = ctx.enter_context(tc.psum_pool(name="w_banks", bufs=2))

        y_rows = {}
        w_rows = {}
        y_words = {}
        stats = {}
        chain = {}
        scale = {}
        shift = {}
        planes = {}
        a_grouped = {}
        y_codes = {}
        y_scales = {}
        w_grouped = {}
        w_codes = {}
        w_scales = {}

        def load(pool, source, r, pieces=1):
            rows = pool.tile([P, ROW_TILES, LOAD_K], BF16, tag="rows")
            width = LOAD_K // pieces
            for first in range(0, LOAD_K, width):
                nc.sync.dma_start(
                    out=rows[:, :, first : first + width],
                    in_=source.rearrange("(t p) k -> p t k", p=P)[
                        :, :, r * LOAD_K + first : r * LOAD_K + first + width
                    ],
                )
            return rows

        def transpose_words(dest, rows, t, g, u):
            first = (g % LOAD_PASSES) * PASS_WORDS
            nc.tensor.transpose(
                dest, rows[:].bitcast(F32)[:, t, first + u : first + PASS_WORDS : HALVES], identity[:]
            )

        def read_words(g):
            r = g // ROUND_PASSES
            if g % ROUND_PASSES == 0:
                six = stat_pool.tile([P, ROUND_PLANES, 2, 6], F32, tag="six")
                stats[r] = six
            words = word_pool.tile([P, HALVES, BATCH], F32, tag="words")
            for u in range(HALVES):
                bank = y_banks.tile([P, BATCH], F32, tag="bank")
                for t in range(ROW_TILES):
                    transpose_words(bank[:, t * P : (t + 1) * P], y_rows[g // LOAD_PASSES], t, g, u)
                nc.scalar.copy(out=words[:, u, :], in_=bank[:])
                values = bank[:].bitcast(BF16)
                for h in range(2):
                    nc.vector.bn_stats(
                        out=stats[r][:, (g % ROUND_PASSES) * HALVES + u, h, :],
                        in_=values[:, h * STATS_MAX : (h + 1) * STATS_MAX],
                    )
            y_words[g] = words

        def spread_gamma_beta():
            bank = w_banks.tile([P, BATCH], F32, tag="bank")
            for u in range(HALVES):
                nc.tensor.transpose(
                    bank[:, u * P : (u + 1) * P], vectors[:].bitcast(F32)[:, u:PASS_WORDS:HALVES], identity[:]
                )
            by_half = bank[:].bitcast(BF16).rearrange("p (u c e) -> p u c e", u=2 * HALVES, e=PAIR)
            for v in range(2):
                for u in range(HALVES):
                    nc.vector.tensor_copy(
                        out=gamma_beta[:, v, u : N_PASS * HALVES : HALVES, :],
                        in_=by_half[:, u, v * N_PASS : (v + 1) * N_PASS, :],
                    )

        def begin_chain(r):
            shape = [P, ROUND_PLANES, PAIR]
            gap = stat_pool.tile(shape, F32, tag="gap")
            twice_mean = stat_pool.tile(shape, F32, tag="twice_mean")
            dev = stat_pool.tile(shape, F32, tag="dev")
            std = stat_pool.tile(shape, F32, tag="std")
            scale_r = affine_pool.tile(shape, F32, tag="scale")
            shift_r = affine_pool.tile(shape, F32, tag="shift")
            chain[r] = gap, twice_mean, dev, std
            scale[r] = scale_r
            shift[r] = shift_r

        def moments(r):
            by_parity = stats[r][:].rearrange("p q h (e s) -> p q h e s", s=3)
            return [by_parity[:, :, h, :, s] for s in (1, 2) for h in range(2)]

        def chain_a(r):
            begin_chain(r)
            mean_a, mean_b, dev_a, dev_b = moments(r)
            gap, twice_mean, dev, std = chain[r]
            nc.vector.tensor_tensor(out=gap[:], in0=mean_a, in1=mean_b, op=ALU.subtract)
            nc.vector.tensor_tensor(out=dev[:], in0=dev_a, in1=dev_b, op=ALU.add)

        def chain_b(r):
            mean_a, mean_b, dev_a, dev_b = moments(r)
            gap, twice_mean, dev, std = chain[r]
            nc.vector.tensor_tensor(out=gap[:], in0=gap[:], in1=gap[:], op=ALU.mult)
            nc.vector.tensor_tensor(out=twice_mean[:], in0=mean_a, in1=mean_b, op=ALU.add)

        def chain_c(r):
            gap, twice_mean, dev, std = chain[r]
            nc.vector.scalar_tensor_tensor(
                out=dev[:], in0=dev[:], scalar=1.0 / 128.0, in1=gap[:], op0=ALU.mult, op1=ALU.add
            )

        def chain_sqrt(r):
            gap, twice_mean, dev, std = chain[r]
            nc.scalar.activation(out=std[:], in_=dev[:], func=ACT.Sqrt, scale=0.25, bias=eps[:])

        def chain_d(r):
            gap, twice_mean, dev, std = chain[r]
            nc.vector.reciprocal(out=std[:], in_=std[:])

        def chain_e(r):
            gap, twice_mean, dev, std = chain[r]
            gamma_r = gamma_beta[:, 0, r * ROUND_PLANES : (r + 1) * ROUND_PLANES, :]
            nc.vector.tensor_tensor(out=scale[r][:], in0=std[:], in1=gamma_r, op=ALU.mult)

        def chain_f(r):
            gap, twice_mean, dev, std = chain[r]
            nc.vector.scalar_tensor_tensor(
                out=gap[:].rearrange("p q e -> p (q e)"),
                in0=twice_mean[:].rearrange("p q e -> p (q e)"),
                scalar=0.5,
                in1=scale[r][:].rearrange("p q e -> p (q e)"),
                op0=ALU.mult,
                op1=ALU.mult,
            )

        def chain_g(r):
            gap, twice_mean, dev, std = chain[r]
            beta_r = gamma_beta[:, 1, r * ROUND_PLANES : (r + 1) * ROUND_PLANES, :]
            nc.vector.tensor_tensor(out=shift[r][:], in0=beta_r, in1=gap[:], op=ALU.subtract)

        links = {
            (0, 0): (chain_a,),
            (0, 1): (chain_b,),
            (0, 2): (chain_c,),
            (1, 0): (chain_d,),
            (1, 1): (chain_e,),
            (1, 2): (chain_f,),
            (2, 0): (chain_g,),
        }

        def run_links(g_stats, slot):
            for late in range(3):
                g = g_stats - late
                if 0 <= g < N_PASS and g % ROUND_PASSES == ROUND_PASSES - 1:
                    for link in links.get((late, slot), ()):
                        link(g // ROUND_PASSES)

        def scale_shift(g, u, e):
            r = g // ROUND_PASSES
            q = (g % ROUND_PASSES) * HALVES + u
            return scale[r][:, q, e : e + 1], shift[r][:, q, e : e + 1]

        def begin_planes(g):
            a_planes = stage.tile([P, PACK, BATCH], BF16, tag="a_planes")
            planes[g] = a_planes

        def word_values(g, u, e):
            return y_words[g][:].bitcast(BF16).rearrange("p u (b e) -> p u b e", e=PAIR)[:, u, :, e]

        def normalise_scalar(g):
            for t in range(SCALAR_PLANES):
                u, e = divmod(t, PAIR)
                by, to = scale_shift(g, u, e)
                nc.scalar.activation(
                    out=planes[g][:, t, :], in_=word_values(g, u, e), func=ACT.Relu, scale=by, bias=to
                )

        def normalise_vector(g):
            for t in range(SCALAR_PLANES, PACK):
                u, e = divmod(t, PAIR)
                by, to = scale_shift(g, u, e)
                nc.vector.tensor_scalar(
                    out=planes[g][:, t, :],
                    in0=word_values(g, u, e),
                    scalar1=by,
                    scalar2=to,
                    op0=ALU.mult,
                    op1=ALU.add,
                )

        def regroup_views(g, first, last):
            return (
                a_grouped[g][:, first:last, :].rearrange("p (c j) t -> p c t j", j=RUN),
                planes[g][:, :, first:last].rearrange("p t (c j) -> p c t j", j=RUN),
            )

        def beside_statistics(g):
            return g + PACK_LAG + STATS_LEAD < N_PASS

        def regroup_gpsimd(g):
            grouped = group_pool.tile([P, BATCH, PACK], BF16, tag="grouped", align_bytes=64)
            a_grouped[g] = grouped
            if not beside_statistics(g):
                return
            dest, source = regroup_views(g, 0, GPSIMD_ROWS)
            nc.gpsimd.tensor_scalar(
                out=dest, in0=source, scalar1=BF16_MAX, scalar2=0.0, op0=ALU.min, op1=ALU.max
            )

        def regroup_vector(g):
            dest, source = regroup_views(g, GPSIMD_ROWS if beside_statistics(g) else 0, BATCH)
            nc.vector.tensor_scalar_max(out=dest, in0=source, scalar1=0.0)

        def copy_weights(g):
            grouped = stage.tile([P, WIDTH * PACK], BF16, tag="w_grouped", align_bytes=64)
            words = grouped[:].bitcast(F32).rearrange("p (o u) -> p o u", u=HALVES)
            rows_in_bank = WIDTH // 2
            for h in range(2):
                bank = w_banks.tile([P, BATCH], F32, tag="bank")
                by_half = bank[:].rearrange("p (u o) -> p u o", u=HALVES)
                for u in range(HALVES):
                    for j in range(rows_in_bank // P):
                        transpose_words(
                            by_half[:, u, j * P : (j + 1) * P], w_rows[g // LOAD_PASSES], 2 * h + j, g, u
                        )
                nc.scalar.copy(
                    out=words[:, h * rows_in_bank : (h + 1) * rows_in_bank, :],
                    in_=by_half.rearrange("p u o -> p o u"),
                )
            w_grouped[g] = grouped

        def quantise(pool, grouped, width, tag):
            codes = pool.tile([P, width], U32, tag=tag + "_codes", align_bytes=64)
            scales = pool.tile([P, width], U8, tag=tag + "_scales", align_bytes=64)
            nc.vector.quantize_mx(out=codes[:].bitcast(FP8X4), scales=scales[:], in_=grouped)
            return codes, scales

        def multiply(g):
            for t in range(ROW_TILES):
                rows = slice(t * P, (t + 1) * P)
                nc.tensor.matmul_mx(
                    out=acc[t][:],
                    lhsT=y_codes[g][:, rows].bitcast(FP8X4),
                    lhsT_scale=y_scales[g][:, rows],
                    rhs=w_codes[g][:].bitcast(FP8X4),
                    rhs_scale=w_scales[g][:],
                    start=(g == 0),
                    stop=(g == N_PASS - 1),
                )

        y_rows[0] = load(y_pool, y_lin, 0, pieces=LOAD_PASSES)
        identity = const.tile([P, P], F32)
        make_identity(nc, identity[:])
        vectors = const.tile([P, K_PASS], BF16)
        nc.gpsimd.memset(vectors[2 * N_PASS : P, :], 0.0)
        nc.sync.dma_start(out=vectors[0:N_PASS, :], in_=gamma.rearrange("(r c) -> r c", c=K_PASS))
        nc.sync.dma_start(out=vectors[N_PASS : 2 * N_PASS, :], in_=beta.rearrange("(r c) -> r c", c=K_PASS))
        y_rows[1] = load(y_pool, y_lin, 1)
        for r in range(LOAD_AHEAD):
            w_rows[r] = load(w_pool, W2, r)
        one = const.tile([P, 1], F32)
        nc.vector.memset(one[:], 1.0)
        eps = const.tile([P, 1], F32)
        nc.vector.tensor_scalar(out=eps[:], in0=one[:], scalar1=BN_EPS, scalar2=None, op0=ALU.mult)
        nc.scalar.activation(out=one[:], in_=one[:], func=ACT.Sqrt)
        gamma_beta = const.tile([P, 2, N_PASS * HALVES, PAIR], F32)
        acc = [acc_pool.tile([P, WIDTH], F32, name="acc%d" % t) for t in range(ROW_TILES)]

        for i in range(-STATS_LEAD, N_PASS + MATMUL_LAG):
            g_stats = i + STATS_LEAD
            g_weight = i + WEIGHT_LEAD
            g_pack = i - PACK_LAG
            g_w = g_pack + WEIGHT_LEAD
            if 0 <= g_pack < N_PASS:
                regroup_gpsimd(g_pack)
            if g_stats < N_PASS:
                r = g_stats // LOAD_PASSES + LOAD_AHEAD
                if g_stats % LOAD_PASSES == 0 and r < N_LOADS:
                    y_rows[r] = load(y_pool, y_lin, r)
                read_words(g_stats)
                if g_stats == 0:
                    spread_gamma_beta()
            if g_stats % ROUND_PASSES == 0 and ROUND_PASSES <= g_stats <= N_PASS:
                chain_sqrt(g_stats // ROUND_PASSES - 1)
            r = g_weight // LOAD_PASSES + LOAD_AHEAD
            if g_weight % LOAD_PASSES == 0 and 0 <= r < N_LOADS:
                w_rows[r] = load(w_pool, W2, r)
            if 0 <= g_weight < N_PASS:
                copy_weights(g_weight)
            if 0 <= g_pack < N_PASS:
                regroup_vector(g_pack)
            run_links(g_stats, 0)
            if 0 <= g_w < N_PASS:
                w_codes[g_w], w_scales[g_w] = quantise(w_mx, w_grouped[g_w][:], WIDTH, "w")
            run_links(g_stats, 1)
            late = 0 <= i < N_PASS and g_stats >= N_PASS
            if late:
                begin_planes(i)
                normalise_vector(i)
            if 0 <= g_pack < N_PASS:
                y_codes[g_pack], y_scales[g_pack] = quantise(
                    y_mx, a_grouped[g_pack][:].rearrange("p b t -> p (b t)"), BATCH, "y"
                )
            run_links(g_stats, 2)
            if 0 <= i < N_PASS:
                if not late:
                    begin_planes(i)
                normalise_scalar(i)
                if not late:
                    normalise_vector(i)
            if 0 <= i - MATMUL_LAG:
                multiply(i - MATMUL_LAG)

        bias_rows = const.tile([P, WIDTH], BF16)
        nc.sync.dma_start(out=bias_rows[:], in_=b2.partition_broadcast(P))
        logits = {}
        norms = {}

        def add_bias(t):
            p_rows = tail.tile([P, WIDTH], F32, tag="p_rows")
            nc.vector.tensor_tensor(out=p_rows[:], in0=acc[t][:], in1=bias_rows[:], op=ALU.add)
            squares = tail.tile([P, WIDTH], F32, tag="squares")
            norm = tail.tile([P, 1], F32, tag="norm")
            nc.scalar.activation(out=squares[:], in_=p_rows[:], func=ACT.Square, accum_out=norm[:])
            nc.scalar.activation(out=norm[:], in_=norm[:], func=ACT.Sqrt)
            logits[t] = p_rows
            norms[t] = norm

        def divide_by_norm(t):
            nc.vector.tensor_scalar_max(out=norms[t][:], in0=norms[t][:], scalar1=L2_EPS)
            nc.vector.reciprocal(out=norms[t][:], in_=norms[t][:])
            nc.vector.tensor_scalar_mul(out=logits[t][:], in0=logits[t][:], scalar1=norms[t][:])
            nc.sync.dma_start(out=out[t * P : (t + 1) * P, :], in_=logits[t][:])

        for t in range(ROW_TILES + 2):
            if t < ROW_TILES:
                add_bias(t)
            if t >= 2:
                divide_by_norm(t - 2)
